import numpy as np
import ml_dtypes


def mxq(x, axis, fmt="e4m3"):
    dtype, down = {"e4m3": (ml_dtypes.float8_e4m3fn, 7), "e5m2": (ml_dtypes.float8_e5m2, 14)}[fmt]
    v = np.moveaxis(np.asarray(x, np.float32).astype(ml_dtypes.bfloat16).astype(np.float64), axis, -1)
    blocks = v.reshape(v.shape[:-1] + (-1, 32))
    amax = np.abs(blocks).max(-1, keepdims=True)
    byte = np.maximum(np.where(amax > 0, np.frexp(amax)[1] - 1 + 127, 0) - down, 1)
    scale = np.exp2(byte - 127.0)
    codes = (blocks / scale).astype(np.float32).astype(dtype).astype(np.float64)
    return np.moveaxis((codes * scale).reshape(v.shape), -1, axis)


WIDE = False


def mx_kscale(k):
    if not WIDE:
        return np.ones(k)
    levels = np.array([18, -18])
    if k % 512:
        return np.exp2(np.random.permutation(np.resize(levels, k // 32))).repeat(32)
    a = np.empty((k // 512, 16))
    for p in range(k // 512):
        a[p, :8] = np.random.permutation(np.resize(levels, 8))
        for g in range(8):
            far = levels[np.abs(levels - a[p, g]) >= 10]
            a[p, g + 8] = far[np.random.randint(len(far))]
    return np.exp2(a.ravel()).repeat(32)


BF16 = ml_dtypes.bfloat16


def bf(x):
    return np.asarray(x, np.float32).astype(BF16)


def f64(x):
    return np.asarray(x).astype(np.float64)


B, S, D, H = 1, 512, 2048, 4
DH = D // H
HALF = DH // 2
ROPE_BASE = 10000.0


def rope_tables():
    inv_freq = 1.0 / ROPE_BASE ** (np.arange(HALF) * 2.0 / DH)
    ang = np.arange(S)[:, None] * inv_freq[None, :]
    return np.cos(ang), np.sin(ang)


def rope_back(g, cos, sin):
    c = cos[None, :, None, :]
    s = sin[None, :, None, :]
    gp = g.reshape(B, S, H, HALF, 2)
    gr, gi = gp[..., 0], gp[..., 1]
    return np.stack([gr * c + gi * s, gi * c - gr * s], axis=-1).reshape(B, S, H, DH)


def setup_inputs():
    s = mx_kscale(B * S).reshape(B, S)
    u = mx_kscale(DH)
    v = np.repeat(mx_kscale(D)[::2], 2)
    q0 = bf(np.random.standard_normal((B, S, D)))
    Wq0 = bf(np.random.standard_normal((D, D)) / np.sqrt(D))
    bq = bf(np.random.standard_normal(D) * 0.1)
    G0 = bf(np.random.standard_normal((H, DH, DH)) / np.sqrt(DH))
    g = bf(np.random.standard_normal((B, H, S, DH)) * np.exp2(np.random.randint(-6, 1, (B, 1, S, 1))) * 4.0 / s[:, None, :, None] * u)
    cos, sin = rope_tables()
    return {"q": bf(f64(q0) * s[:, :, None]),
            "Wq": bf(f64(Wq0) / v[:, None]),
            "bq": bq,
            "G": bf(f64(G0) * v.reshape(H, DH)[:, :, None] / u[None, None, :]),
            "rope_cos": np.asarray(cos, np.float32),
            "rope_sin": np.asarray(sin, np.float32),
            "grad_out": g}


def reference(q, Wq, bq, G, rope_cos, rope_sin, grad_out):
    dr = mxq(f64(grad_out), 3, "e5m2") @ mxq(f64(G), 2, "e4m3").transpose(0, 2, 1)
    dqp = rope_back(dr.transpose(0, 2, 1, 3), f64(rope_cos), f64(rope_sin)).reshape(B * S, D)
    dq = (mxq(dqp, 1, "e5m2") @ mxq(f64(Wq), 0, "e4m3")).reshape(B, S, D)
    dWq = mxq(dqp, 0, "e5m2").T @ mxq(f64(q).reshape(B * S, D), 0, "e4m3")
    return dq, dWq

@@ -1,0 +1,364 @@
+from contextlib import ExitStack
+
+import concourse.mybir as mybir
+from concourse.masks import make_identity
+
+S, D, H, DH = 512, 2048, 4, 512
+FLOPS = 2 * S * D * DH + 2 * 2 * S * D * D
+BYTES = 2 * (S * D + D * D + H * DH * DH + H * S * DH) + 4 * (S * DH + S * D + D * D)
+
+F32 = mybir.dt.float32
+BF16 = mybir.dt.bfloat16
+U32 = mybir.dt.uint32
+U8 = mybir.dt.uint8
+E4M3 = mybir.dt.float8_e4m3fn_x4
+E5M2 = mybir.dt.float8_e5m2_x4
+MULT = mybir.AluOpType.mult
+ADD = mybir.AluOpType.add
+SUB = mybir.AluOpType.subtract
+
+P = 128
+PACK = 4
+NT = 512
+PAIRS = DH // 2
+
+
+def tile_plgmultiheadattention_pa_v_kernel(tc, q, Wq, bq, G, rope_cos, rope_sin, grad_out, out_0, out_1):
+    nc = tc.nc
+
+    go_view = grad_out.rearrange("b h (p j) e -> (b h) p j e", j=PACK)
+    g_view = G.rearrange("h (r m) e -> h r m e", m=PACK)
+    cos_view = rope_cos.rearrange("(p j) i -> p j i", j=PACK)
+    sin_view = rope_sin.rearrange("(p j) i -> p j i", j=PACK)
+    q_view = q.rearrange("b (p j) c -> (b p) j c", j=PACK)
+    w_view = Wq.rearrange("(g p e u) c -> g u p e c", g=H, e=2, u=2)
+    dw_view = out_1.rearrange("(h a i u) c -> h u a i c", h=H, a=2, u=2)
+    dq_view = out_0.rearrange("b (p j) c -> j (b p) c", j=PACK)
+
+    with ExitStack() as ctx:
+        keep = ctx.enter_context(tc.tile_pool(name="keep", bufs=1))
+        sb = ctx.enter_context(tc.tile_pool(name="sb", bufs=2))
+        psum = ctx.enter_context(tc.psum_pool(name="psum", bufs=2))
+        ctx.enter_context(tc.manual_schedule())
+
+        ident = keep.tile([P, P], F32, name="ident")
+        tab = keep.tile([P, 2, PACK, PAIRS], F32, name="tab")
+        q_codes = keep.tile([P, D], U32, name="q_codes", align_bytes=64)
+        q_scales = keep.tile([P, D], U8, name="q_scales", align_bytes=64)
+        w_codes = keep.tile([P, H, D], U32, name="w_codes", align_bytes=64)
+        w_scales = keep.tile([P, H, D], U8, name="w_scales", align_bytes=64)
+        f_codes = keep.tile([P, H, S], U32, name="f_codes", align_bytes=64)
+        f_scales = keep.tile([P, H, S], U8, name="f_scales", align_bytes=64)
+
+        raw = {}
+
+        def load_head(h):
+            t = sb.tile([P, 2, PACK, DH], BF16, name="raw8", tag="raw8", bufs=8)
+            nc.sync.dma_start(out=t[:, 0, :, :], in_=go_view[h])
+            nc.sync.dma_start(out=t[:, 1, :, :], in_=g_view[h])
+            raw["go", h] = t[:, 0, :, :]
+            raw["g", h] = t[:, 1, :, :]
+
+        def load_q(half):
+            t = sb.tile([P, PACK, 1024], BF16, name="raw8", tag="raw8", bufs=8)
+            nc.sync.dma_start(out=t[:], in_=q_view[:, :, half * 1024 : half * 1024 + 1024])
+            raw["q", half] = t
+
+        def load_w(half, g, queue=nc.sync):
+            t = sb.tile([P, PACK, 1024], BF16, name="raw8", tag="raw8", bufs=8)
+            for u in range(2):
+                queue.dma_start(
+                    out=t[:, 2 * u : 2 * u + 2, :], in_=w_view[g, u, :, :, half * 1024 : half * 1024 + 1024]
+                )
+            raw["w", half, g] = t
+
+        def copy(engine, out, in_):
+            if engine == "v":
+                nc.vector.tensor_copy(out=out, in_=in_)
+            else:
+                nc.scalar.copy(out=out, in_=in_)
+
+        def bank_of(blocks):
+            bank = psum.tile([P, 4, P], F32, name="tp", tag="tp", bufs=2)
+            for a in range(4):
+                nc.tensor.transpose(bank[:, a, :], blocks[a], ident[:])
+            return bank
+
+        grouped = {}
+        banks = {}
+        codes = {}
+
+        def turn_go(h, b):
+            words = raw["go", h].rearrange("p j e -> p (j e)").bitcast(F32)
+            blocks = [words[:, 256 * (2 * b + jj) + u : 256 * (2 * b + jj) + 256 : 2] for jj in range(2) for u in range(2)]
+            banks["go", b] = bank_of(blocks)
+
+        def out_go(h, b, engine):
+            if b == 0:
+                grouped["go", h] = sb.tile([P, S * PACK], BF16, name="grp_in", tag="grp_in", bufs=3, align_bytes=64)
+            words_out("go", grouped["go", h], b, engine)
+
+        def words_out(name, tile, b, engine):
+            dst = tile[:].bitcast(F32)[:, 512 * b : 512 * b + 512]
+            copy(
+                engine,
+                dst.rearrange("p (j r u) -> p j r u", j=2, u=2),
+                banks[name, b][:].rearrange("p (j u) r -> p j r u", j=2),
+            )
+
+        def turn_g(h, b):
+            words = raw["g", h].rearrange("p m e -> p (m e)").bitcast(F32)
+            blocks = [words[:, 256 * (b + 2 * a) + u : 256 * (b + 2 * a) + 256 : 2] for a in range(2) for u in range(2)]
+            banks["g", b] = bank_of(blocks)
+
+        def out_g(h, b, engine):
+            if b == 0:
+                grouped["g", h] = sb.tile([P, DH * PACK], BF16, name="grp_in", tag="grp_in", bufs=3, align_bytes=64)
+            dst = grouped["g", h][:].bitcast(F32)[:, 512 * b : 512 * b + 512]
+            copy(engine, dst.rearrange("p (r a) -> p r a", a=4), banks["g", b][:].rearrange("p a r -> p r a"))
+
+        def quant(key, dtype, out_codes=None, out_scales=None):
+            nc.vector.quantize_mx(out=out_codes.bitcast(dtype), scales=out_scales, in_=grouped[key][:])
+
+        def quant_in(name, h):
+            c = sb.tile([P, 512], U32, name="c_" + name, tag="c_" + name, bufs=2, align_bytes=64)
+            s = sb.tile([P, 512], U8, name="s_" + name, tag="s_" + name, bufs=2, align_bytes=64)
+            quant((name, h), E5M2 if name == "go" else E4M3, c[:], s[:])
+            codes[name, h] = (c, s)
+
+        dr = {}
+
+        def stage_one(h, j):
+            gc, gs = codes["go", h]
+            mc, ms = codes["g", h]
+            bank = psum.tile([P, NT], F32, name="dr", tag="dr", bufs=3)
+            cols = slice(P * j, P * j + P)
+            nc.tensor.matmul_mx(
+                out=bank[:], lhsT=gc[:, cols].bitcast(E5M2), lhsT_scale=gs[:, cols],
+                rhs=mc[:].bitcast(E4M3), rhs_scale=ms[:], start=True, stop=True,
+            )
+            dr[h, j] = bank
+
+        prods = {}
+        dqp = {}
+
+        def products(h, j):
+            if j == 0:
+                prods[h] = sb.tile([P, PACK, 2, 2, PAIRS], F32, name="prods", tag="prods", bufs=1)
+            bank = dr[h, j][:].rearrange("p (u i) -> p u i", u=2)
+            nc.vector.tensor_tensor(
+                out=prods[h][:, j, :, :, :],
+                in0=bank.unsqueeze(1).to_broadcast([P, 2, 2, PAIRS]),
+                in1=tab[:, :, j, :].unsqueeze(2).to_broadcast([P, 2, 2, PAIRS]),
+                op=MULT,
+            )
+
+        def combine(h, j, engine):
+            if j == 0:
+                dqp[h] = sb.tile([P, PACK, 2, PAIRS], BF16, name="dqp", tag="dqp", bufs=2)
+            pr = prods[h]
+            e = nc.gpsimd if engine == "g" else nc.vector
+            for u in range(2):
+                e.tensor_tensor(
+                    out=dqp[h][:, j, u, :], in0=pr[:, j, 0, u, :], in1=pr[:, j, 1, 1 - u, :], op=ADD if u == 0 else SUB
+                )
+
+        def group_tokens(h, engine):
+            grouped["tok", h] = sb.tile([P, DH * PACK], BF16, name="grp_d", tag="grp_d", bufs=3, align_bytes=64)
+            copy(
+                engine,
+                grouped["tok", h][:].rearrange("p (d j) -> p d j", j=PACK),
+                dqp[h][:].rearrange("p j u i -> p (u i) j"),
+            )
+
+        def quant_tokens(h):
+            c = sb.tile([P, 512], U32, name="c_tok", tag="c_tok", bufs=4, align_bytes=64)
+            s = sb.tile([P, 512], U8, name="s_tok", tag="s_tok", bufs=4, align_bytes=64)
+            quant(("tok", h), E5M2, c[:], s[:])
+            codes["tok", h] = (c, s)
+
+        def turn_dqp(h, b):
+            words = dqp[h][:].rearrange("p j u i -> p (j u i)").bitcast(F32)
+            banks["f", b] = bank_of([words[:, P * (4 * b + a) : P * (4 * b + a) + P] for a in range(4)])
+
+        def out_dqp(h, b, engine):
+            if b == 0:
+                grouped["f", h] = sb.tile([P, S * PACK], BF16, name="grp_d", tag="grp_d", bufs=3, align_bytes=64)
+            words_out("f", grouped["f", h], b, engine)
+
+        def quant_features(h):
+            quant(("f", h), E5M2, f_codes[:, h, :], f_scales[:, h, :])
+
+        def group_q(n, engine):
+            grouped["q", n] = sb.tile([P, NT * PACK], BF16, name="grp_w", tag="grp_w", bufs=3, align_bytes=64)
+            src = raw["q", n // 2][:, :, NT * (n % 2) : NT * (n % 2) + NT]
+            copy(engine, grouped["q", n][:].rearrange("p (c j) -> p c j", j=PACK), src.rearrange("p j c -> p c j"))
+
+        def quant_q(n):
+            cols = slice(NT * n, NT * n + NT)
+            quant(("q", n), E4M3, q_codes[:, cols], q_scales[:, cols])
+
+        def group_w(n, g, engine):
+            grouped["w", n, g] = sb.tile([P, NT * PACK], BF16, name="grp_w", tag="grp_w", bufs=3, align_bytes=64)
+            src = raw["w", n // 2, g][:, :, NT * (n % 2) : NT * (n % 2) + NT]
+            copy(engine, grouped["w", n, g][:].rearrange("p (c s) -> p c s", s=PACK), src.rearrange("p s c -> p c s"))
+
+        def quant_w(n, g):
+            cols = slice(NT * n, NT * n + NT)
+            quant(("w", n, g), E4M3, w_codes[:, g, cols], w_scales[:, g, cols])
+
+        todo = []
+        stage = {}
+
+        def queue_dw(h):
+            for half in range(2):
+                for t in range(4):
+                    for n in range(2):
+                        todo.append((h, half, t, n))
+
+        def dw_tile(h, half, t, n, engine):
+            tc_, ts_ = codes["tok", h]
+            acc = psum.tile([P, NT], F32, name="acc", tag="acc", bufs=3)
+            rows = slice(P * t, P * t + P)
+            cols = slice(1024 * half + NT * n, 1024 * half + NT * n + NT)
+            nc.tensor.matmul_mx(
+                out=acc[:], lhsT=tc_[:, rows].bitcast(E5M2), lhsT_scale=ts_[:, rows],
+                rhs=q_codes[:, cols].bitcast(E4M3), rhs_scale=q_scales[:, cols], start=True, stop=True,
+            )
+            if n == 0:
+                stage[0] = sb.tile([P, 1024], F32, name="stage", tag="stage", bufs=5)
+            copy(engine, stage[0][:, NT * n : NT * n + NT], acc[:])
+            if n == 1:
+                nc.sync.dma_start(
+                    out=dw_view[h, t // 2, t % 2, :, 1024 * half : 1024 * half + 1024], in_=stage[0][:]
+                )
+
+        def pump(count, engine="s"):
+            for i in range(count):
+                if todo:
+                    dw_tile(*todo.pop(0), engine)
+
+        acc0 = {}
+
+        def dq_pass(n, g):
+            for j in range(PACK):
+                if g == 0:
+                    tag = "dr" if j < 3 else "tp"
+                    acc0[j] = psum.tile([P, NT], F32, name=tag, tag=tag, bufs=3 if j < 3 else 2)
+                rows = slice(P * j, P * j + P)
+                cols = slice(NT * n, NT * n + NT)
+                nc.tensor.matmul_mx(
+                    out=acc0[j][:], lhsT=f_codes[:, g, rows].bitcast(E5M2), lhsT_scale=f_scales[:, g, rows],
+                    rhs=w_codes[:, g, cols].bitcast(E4M3), rhs_scale=w_scales[:, g, cols], start=g == 0, stop=g == H - 1,
+                )
+
+        def dq_out(n, engines):
+            for j in range(PACK):
+                t = sb.tile([P, NT], F32, name="stage", tag="stage", bufs=5)
+                copy(engines[j], t[:], acc0[j][:])
+                nc.sync.dma_start(out=dq_view[j, :, NT * n : NT * n + NT], in_=t[:])
+
+        make_identity(nc, ident[:])
+        load_head(0)
+        load_q(0)
+        nc.sync.dma_start(out=tab[:, 0, :, :], in_=cos_view)
+        nc.sync.dma_start(out=tab[:, 1, :, :], in_=sin_view)
+        load_head(1)
+        load_q(1)
+        load_head(2)
+        load_head(3)
+        load_w(0, 0)
+        load_w(0, 1)
+
+        turn_go(0, 0)
+        turn_go(0, 1)
+        out_go(0, 0, "s")
+        out_go(0, 1, "v")
+        turn_g(0, 0)
+        turn_g(0, 1)
+        out_g(0, 0, "s")
+        out_g(0, 1, "v")
+        quant_in("go", 0)
+        quant_in("g", 0)
+        for j in range(3):
+            stage_one(0, j)
+        group_q(0, "v")
+        group_q(1, "s")
+        quant_q(0)
+
+        wsteps = [(n, g) for n in range(4) for g in range(H)]
+        for h in range(H):
+            last = h == H - 1
+            products(h, 0)
+            stage_one(h, 3)
+            combine(h, 0, "g")
+            if not last:
+                turn_go(h + 1, 0)
+                turn_go(h + 1, 1)
+                out_go(h + 1, 0, "s")
+                out_go(h + 1, 1, "s")
+            pump(2)
+            products(h, 1)
+            combine(h, 1, "g")
+            if not last:
+                turn_g(h + 1, 0)
+                turn_g(h + 1, 1)
+            pump(2)
+            if h == 0:
+                group_q(2, "s")
+            products(h, 2)
+            combine(h, 2, "g")
+            pump(2)
+            products(h, 3)
+            combine(h, 3, "g")
+            if not last:
+                out_g(h + 1, 0, "v")
+                out_g(h + 1, 1, "v")
+            turn_dqp(h, 0)
+            out_dqp(h, 0, "s")
+            pump(2)
+            if h > 0:
+                quant_features(h - 1)
+            if h < 2:
+                quant_q(1 + 2 * h)
+            if not last:
+                quant_in("go", h + 1)
+            turn_dqp(h, 1)
+            out_dqp(h, 1, "s")
+            if h == 0:
+                group_q(3, "s")
+            group_tokens(h, "v")
+            pump(2)
+            if not last:
+                quant_in("g", h + 1)
+            if h == 0:
+                quant_q(2)
+            quant_tokens(h)
+            pump(2)
+            if not last:
+                for j in range(3):
+                    stage_one(h + 1, j)
+            queue_dw(h)
+            if h == 0:
+                load_w(0, 2)
+                load_w(0, 3)
+            if h == 1:
+                load_w(1, 0)
+                load_w(1, 1)
+            if h == 2:
+                load_w(1, 2)
+                load_w(1, 3)
+        group_w(0, 0, "v")
+        quant_features(3)
+        for k in range(16):
+            n, g = wsteps[k]
+            if k < 15:
+                nn, ng = wsteps[k + 1]
+                group_w(nn, ng, "v")
+            pump(1)
+            quant_w(n, g)
+            pump(2)
+            dq_pass(n, g)
+            if g == 3:
+                dq_out(n, "ssss" if n < 3 else "svsv")
+        pump(100)

@@ -18,9 +18,23 @@ ADD = mybir.AluOpType.add
 SUB = mybir.AluOpType.subtract
 
 P = 128
+KIB = 1024
 PACK = 4
 NT = 512
 PAIRS = DH // 2
+
+ADDS = ["gggv","gggv","gvgv","gggv"]
+ORDER = (
+    "L L L L L L L T T Ts Ts T T T Ts Ts Qs T P P P P P P P P P P P P K K T T Ts Ts T T Qs T "
+    "Q Ts Ts Qs Q M Qs M M T P P P P P P P P P P P P K K T T X X Ts Ts F Fs X X X F Fs X T T "
+    "Q Q Es M T Ts X X X Ts X X F F Fs F Fs F Es M Es M Es Es M M Es M T P P P P P P P P P P P "
+    "P K K T T Ts Ts T T X Es M Es M Es Es M M T Ts Ts F Fs F Fv X X Es M Es M Es M Es M T P P P P "
+    "P P P P P P P P K K Es M Ws X X Es M Es M Es M Es M Es M Es M Es M Es M Es M F F Fv F Fv F Es "
+    "M Es Es Es M M M Es M Es M Es M Es M Es M Es M Es M Es M Wv W O Es M Es M Es M Wv W O Wv Es M Es M "
+    "Es M Es M Es M Es M W O Wv Es M Es M Es M W O Zs Zs Zs Zs Wv W O Wv W O Wv Es M Es Es Es M M M Es M "
+    "Es M Es M W O Wv Es M Es M Es M W O Zs Zs Zs Zs Wv W O Wv W O Es M Es M Es M Es Es Es Wv W O Wv W O "
+    "Zs Zs Zs Zs Wv W O Wv W O Wv W O W O Zs Zs Zs Zs "
+)
 
 
 def tile_plgmultiheadattention_pa_v_kernel(tc, q, Wq, bq, G, rope_cos, rope_sin, grad_out, out_0, out_1):
@@ -31,12 +45,13 @@ def tile_plgmultiheadattention_pa_v_kernel(tc, q, Wq, bq, G, rope_cos, rope_sin,
     cos_view = rope_cos.rearrange("(p j) i -> p j i", j=PACK)
     sin_view = rope_sin.rearrange("(p j) i -> p j i", j=PACK)
     q_view = q.rearrange("b (p j) c -> (b p) j c", j=PACK)
-    w_view = Wq.rearrange("(g p e u) c -> g u p e c", g=H, e=2, u=2)
+    w_view = Wq.rearrange("(g p j) c -> g p j c", g=H, j=PACK)
     dw_view = out_1.rearrange("(h a i u) c -> h u a i c", h=H, a=2, u=2)
     dq_view = out_0.rearrange("b (p j) c -> j (b p) c", j=PACK)
 
     with ExitStack() as ctx:
         keep = ctx.enter_context(tc.tile_pool(name="keep", bufs=1))
+        region = ctx.enter_context(tc.tile_pool(name="region", bufs=1))
         sb = ctx.enter_context(tc.tile_pool(name="sb", bufs=2))
         psum = ctx.enter_context(tc.psum_pool(name="psum", bufs=2))
         ctx.enter_context(tc.manual_schedule())
@@ -53,24 +68,33 @@ def tile_plgmultiheadattention_pa_v_kernel(tc, q, Wq, bq, G, rope_cos, rope_sin,
         raw = {}
 
         def load_head(h):
-            t = sb.tile([P, 2, PACK, DH], BF16, name="raw8", tag="raw8", bufs=8)
-            nc.sync.dma_start(out=t[:, 0, :, :], in_=go_view[h])
+            name = "head%d" % h
+            t = region.tile([P, 2, PACK, DH], BF16, name=name, tag=name, offset=KIB * (32 + 8 * h))
+            if h == 0:
+                nc.sync.dma_start(out=t[:, 0, 0:2, :], in_=go_view[h, :, 0:2, :])
+                nc.sync.dma_start(out=t[:, 0, 2:4, :], in_=go_view[h, :, 2:4, :])
+            else:
+                nc.sync.dma_start(out=t[:, 0, :, :], in_=go_view[h])
             nc.sync.dma_start(out=t[:, 1, :, :], in_=g_view[h])
             raw["go", h] = t[:, 0, :, :]
             raw["g", h] = t[:, 1, :, :]
 
         def load_q(half):
-            t = sb.tile([P, PACK, 1024], BF16, name="raw8", tag="raw8", bufs=8)
+            name = "q%d" % half
+            t = region.tile([P, PACK, 1024], BF16, name=name, tag=name, offset=KIB * 8 * half)
             nc.sync.dma_start(out=t[:], in_=q_view[:, :, half * 1024 : half * 1024 + 1024])
             raw["q", half] = t
 
-        def load_w(half, g, queue=nc.sync):
-            t = sb.tile([P, PACK, 1024], BF16, name="raw8", tag="raw8", bufs=8)
-            for u in range(2):
-                queue.dma_start(
-                    out=t[:, 2 * u : 2 * u + 2, :], in_=w_view[g, u, :, :, half * 1024 : half * 1024 + 1024]
-                )
-            raw["w", half, g] = t
+        def load_w(g, j):
+            if j == 0:
+                name = "w%d" % g
+                place = (0, 1, 2, 3)[g]
+                raw["w", g] = region.tile([P, PACK, D], BF16, name=name, tag=name, offset=KIB * 16 * place)
+            nc.sync.dma_start(out=raw["w", g][:, j, :], in_=w_view[g, :, j, :])
+
+        def load_tab():
+            nc.sync.dma_start(out=tab[:, 0, :, :], in_=cos_view)
+            nc.sync.dma_start(out=tab[:, 1, :, :], in_=sin_view)
 
         def copy(engine, out, in_):
             if engine == "v":
@@ -95,7 +119,7 @@ def tile_plgmultiheadattention_pa_v_kernel(tc, q, Wq, bq, G, rope_cos, rope_sin,
 
         def out_go(h, b, engine):
             if b == 0:
-                grouped["go", h] = sb.tile([P, S * PACK], BF16, name="grp_in", tag="grp_in", bufs=3, align_bytes=64)
+                grouped["go", h] = sb.tile([P, S * PACK], BF16, name="grp_in", tag="grp_in", bufs=2, align_bytes=64)
             words_out("go", grouped["go", h], b, engine)
 
         def words_out(name, tile, b, engine):
@@ -113,7 +137,7 @@ def tile_plgmultiheadattention_pa_v_kernel(tc, q, Wq, bq, G, rope_cos, rope_sin,
 
         def out_g(h, b, engine):
             if b == 0:
-                grouped["g", h] = sb.tile([P, DH * PACK], BF16, name="grp_in", tag="grp_in", bufs=3, align_bytes=64)
+                grouped["g", h] = sb.tile([P, DH * PACK], BF16, name="grp_in", tag="grp_in", bufs=2, align_bytes=64)
             dst = grouped["g", h][:].bitcast(F32)[:, 512 * b : 512 * b + 512]
             copy(engine, dst.rearrange("p (r a) -> p r a", a=4), banks["g", b][:].rearrange("p a r -> p r a"))
 
@@ -144,7 +168,7 @@ def tile_plgmultiheadattention_pa_v_kernel(tc, q, Wq, bq, G, rope_cos, rope_sin,
 
         def products(h, j):
             if j == 0:
-                prods[h] = sb.tile([P, PACK, 2, 2, PAIRS], F32, name="prods", tag="prods", bufs=1)
+                prods[h] = region.tile([P, PACK, 2, 2, PAIRS], F32, name="prods", tag="prods", offset=KIB * 64)
             bank = dr[h, j][:].rearrange("p (u i) -> p u i", u=2)
             nc.vector.tensor_tensor(
                 out=prods[h][:, j, :, :, :],
@@ -200,165 +224,91 @@ def tile_plgmultiheadattention_pa_v_kernel(tc, q, Wq, bq, G, rope_cos, rope_sin,
 
         def group_w(n, g, engine):
             grouped["w", n, g] = sb.tile([P, NT * PACK], BF16, name="grp_w", tag="grp_w", bufs=3, align_bytes=64)
-            src = raw["w", n // 2, g][:, :, NT * (n % 2) : NT * (n % 2) + NT]
-            copy(engine, grouped["w", n, g][:].rearrange("p (c s) -> p c s", s=PACK), src.rearrange("p s c -> p c s"))
+            src = raw["w", g][:, :, NT * n : NT * n + NT]
+            copy(
+                engine,
+                grouped["w", n, g][:].rearrange("p (c u e) -> p c u e", u=2, e=2),
+                src.rearrange("p (e u) c -> p c u e", e=2),
+            )
 
         def quant_w(n, g):
             cols = slice(NT * n, NT * n + NT)
             quant(("w", n, g), E4M3, w_codes[:, g, cols], w_scales[:, g, cols])
 
-        todo = []
         stage = {}
+        accs = {}
 
-        def queue_dw(h):
-            for half in range(2):
-                for t in range(4):
-                    for n in range(2):
-                        todo.append((h, half, t, n))
-
-        def dw_tile(h, half, t, n, engine):
+        def dw_mm(h, t, c, first, width):
             tc_, ts_ = codes["tok", h]
             acc = psum.tile([P, NT], F32, name="acc", tag="acc", bufs=3)
             rows = slice(P * t, P * t + P)
-            cols = slice(1024 * half + NT * n, 1024 * half + NT * n + NT)
+            cols = slice(c, c + NT)
             nc.tensor.matmul_mx(
                 out=acc[:], lhsT=tc_[:, rows].bitcast(E5M2), lhsT_scale=ts_[:, rows],
                 rhs=q_codes[:, cols].bitcast(E4M3), rhs_scale=q_scales[:, cols], start=True, stop=True,
             )
-            if n == 0:
-                stage[0] = sb.tile([P, 1024], F32, name="stage", tag="stage", bufs=5)
-            copy(engine, stage[0][:, NT * n : NT * n + NT], acc[:])
-            if n == 1:
-                nc.sync.dma_start(
-                    out=dw_view[h, t // 2, t % 2, :, 1024 * half : 1024 * half + 1024], in_=stage[0][:]
-                )
+            accs[h, t, c] = acc
 
-        def pump(count, engine="s"):
-            for i in range(count):
-                if todo:
-                    dw_tile(*todo.pop(0), engine)
+        def dw_out(h, t, c, first, width, engine):
+            if c == first:
+                stage[0] = sb.tile([P, width], F32, name="stage", tag="stage", bufs=3)
+            copy(engine, stage[0][:, c - first : c - first + NT], accs[h, t, c][:])
+            if c + NT == first + width:
+                nc.sync.dma_start(out=dw_view[h, t // 2, t % 2, :, first : first + width], in_=stage[0][:])
 
         acc0 = {}
 
-        def dq_pass(n, g):
+        def dq_mm(n, g):
             for j in range(PACK):
-                if g == 0:
+                if g == 1:
                     tag = "dr" if j < 3 else "tp"
-                    acc0[j] = psum.tile([P, NT], F32, name=tag, tag=tag, bufs=3 if j < 3 else 2)
+                    acc0[n, j] = psum.tile([P, NT], F32, name=tag, tag=tag, bufs=3 if j < 3 else 2)
                 rows = slice(P * j, P * j + P)
                 cols = slice(NT * n, NT * n + NT)
                 nc.tensor.matmul_mx(
-                    out=acc0[j][:], lhsT=f_codes[:, g, rows].bitcast(E5M2), lhsT_scale=f_scales[:, g, rows],
-                    rhs=w_codes[:, g, cols].bitcast(E4M3), rhs_scale=w_scales[:, g, cols], start=g == 0, stop=g == H - 1,
+                    out=acc0[n, j][:], lhsT=f_codes[:, g, rows].bitcast(E5M2), lhsT_scale=f_scales[:, g, rows],
+                    rhs=w_codes[:, g, cols].bitcast(E4M3), rhs_scale=w_scales[:, g, cols], start=g == 1, stop=g == 3,
                 )
 
-        def dq_out(n, engines):
-            for j in range(PACK):
-                t = sb.tile([P, NT], F32, name="stage", tag="stage", bufs=5)
-                copy(engines[j], t[:], acc0[j][:])
-                nc.sync.dma_start(out=dq_view[j, :, NT * n : NT * n + NT], in_=t[:])
+        def dq_out(n, j, engine):
+            name = "dq%d" % (4 * (n % 2) + j)
+            t = region.tile([P, NT], F32, name=name, tag=name, offset=KIB * (64 + 8 * (n % 2) + 2 * j))
+            copy(engine, t[:], acc0[n, j][:])
+            nc.sync.dma_start(out=dq_view[j, :, NT * n : NT * n + NT], in_=t[:])
 
         make_identity(nc, ident[:])
-        load_head(0)
-        load_q(0)
-        nc.sync.dma_start(out=tab[:, 0, :, :], in_=cos_view)
-        nc.sync.dma_start(out=tab[:, 1, :, :], in_=sin_view)
-        load_head(1)
-        load_q(1)
-        load_head(2)
-        load_head(3)
-        load_w(0, 0)
-        load_w(0, 1)
-
-        turn_go(0, 0)
-        turn_go(0, 1)
-        out_go(0, 0, "s")
-        out_go(0, 1, "v")
-        turn_g(0, 0)
-        turn_g(0, 1)
-        out_g(0, 0, "s")
-        out_g(0, 1, "v")
-        quant_in("go", 0)
-        quant_in("g", 0)
-        for j in range(3):
-            stage_one(0, j)
-        group_q(0, "v")
-        group_q(1, "s")
-        quant_q(0)
-
-        wsteps = [(n, g) for n in range(4) for g in range(H)]
+        gs = (1, 2, 0, 3)
+        steps = {
+            "L": [(load_head, 0)] + [(load_tab,), (load_q, 0), (load_head, 1), (load_q, 1)] + [(load_head, 2), (load_head, 3)],
+            "T": [], "P": [], "K": [], "F": [], "Q": [], "W": [], "M": [], "E": [], "O": [], "Z": [], "X": [],
+        }
         for h in range(H):
-            last = h == H - 1
-            products(h, 0)
-            stage_one(h, 3)
-            combine(h, 0, "g")
-            if not last:
-                turn_go(h + 1, 0)
-                turn_go(h + 1, 1)
-                out_go(h + 1, 0, "s")
-                out_go(h + 1, 1, "s")
-            pump(2)
-            products(h, 1)
-            combine(h, 1, "g")
-            if not last:
-                turn_g(h + 1, 0)
-                turn_g(h + 1, 1)
-            pump(2)
-            if h == 0:
-                group_q(2, "s")
-            products(h, 2)
-            combine(h, 2, "g")
-            pump(2)
-            products(h, 3)
-            combine(h, 3, "g")
-            if not last:
-                out_g(h + 1, 0, "v")
-                out_g(h + 1, 1, "v")
-            turn_dqp(h, 0)
-            out_dqp(h, 0, "s")
-            pump(2)
-            if h > 0:
-                quant_features(h - 1)
-            if h < 2:
-                quant_q(1 + 2 * h)
-            if not last:
-                quant_in("go", h + 1)
-            turn_dqp(h, 1)
-            out_dqp(h, 1, "s")
-            if h == 0:
-                group_q(3, "s")
-            group_tokens(h, "v")
-            pump(2)
-            if not last:
-                quant_in("g", h + 1)
-            if h == 0:
-                quant_q(2)
-            quant_tokens(h)
-            pump(2)
-            if not last:
-                for j in range(3):
-                    stage_one(h + 1, j)
-            queue_dw(h)
-            if h == 0:
-                load_w(0, 2)
-                load_w(0, 3)
-            if h == 1:
-                load_w(1, 0)
-                load_w(1, 1)
-            if h == 2:
-                load_w(1, 2)
-                load_w(1, 3)
-        group_w(0, 0, "v")
-        quant_features(3)
+            steps["T"] += [(turn_go, h, 0), (turn_go, h, 1), (out_go, h, 0), (out_go, h, 1), (turn_g, h, 0), (turn_g, h, 1)]
+            steps["T"] += [(quant_in, "go", h), (out_g, h, 0), (out_g, h, 1), (quant_in, "g", h)]
+            steps["P"] += [(stage_one, h, 0), (stage_one, h, 1), (stage_one, h, 2)]
+            for j in range(PACK):
+                steps["P"].append((products, h, j))
+                if j == 0:
+                    steps["P"].append((stage_one, h, 3))
+                steps["P"].append((combine, h, j, ADDS[h][j]))
+            steps["K"] += [(group_tokens, h, "v"), (quant_tokens, h)]
+            steps["F"] += [(turn_dqp, h, 0), (out_dqp, h, 0), (turn_dqp, h, 1), (out_dqp, h, 1), (quant_features, h)]
+            width = 1024 if h == 0 else D
+            for first in range(0, D, width):
+                for t in range(4):
+                    for c in range(first, first + width, NT):
+                        steps["M"].append((dw_mm, h, t, c, first, width))
+                        steps["E"].append((dw_out, h, t, c, first, width))
+        steps["Q"] = [(group_q, 0), (group_q, 1), (quant_q, 0), (group_q, 2), (quant_q, 1), (group_q, 3), (quant_q, 2), (quant_q, 3)]
+        ws = [(n, g) for n in range(4) for g in gs]
+        steps["W"].append((group_w,) + ws[0])
         for k in range(16):
-            n, g = wsteps[k]
             if k < 15:
-                nn, ng = wsteps[k + 1]
-                group_w(nn, ng, "v")
-            pump(1)
-            quant_w(n, g)
-            pump(2)
-            dq_pass(n, g)
-            if g == 3:
-                dq_out(n, "ssss" if n < 3 else "svsv")
-        pump(100)
+                steps["W"].append((group_w,) + ws[k + 1])
+            steps["W"].append((quant_w,) + ws[k])
+            steps["O"].append((dq_mm,) + ws[k])
+        steps["Z"] = [(dq_out, n, j) for n in range(4) for j in range(4)]
+        steps["X"] = [(load_w, g, j) for g in gs for j in range(4)]
+        for token in ORDER.split():
+            step = steps[token[0]].pop(0)
+            step[0](*step[1:], *token[1:])

from contextlib import ExitStack

import concourse.mybir as mybir
from concourse.masks import make_identity

S, D, H, DH = 512, 2048, 4, 512
FLOPS = 2 * S * D * DH + 2 * 2 * S * D * D
BYTES = 2 * (S * D + D * D + H * DH * DH + H * S * DH) + 4 * (S * DH + S * D + D * D)

F32 = mybir.dt.float32
BF16 = mybir.dt.bfloat16
U32 = mybir.dt.uint32
U8 = mybir.dt.uint8
E4M3 = mybir.dt.float8_e4m3fn_x4
E5M2 = mybir.dt.float8_e5m2_x4
MULT = mybir.AluOpType.mult
ADD = mybir.AluOpType.add
SUB = mybir.AluOpType.subtract

P = 128
KIB = 1024
PACK = 4
NT = 512
PAIRS = DH // 2

ADDS = ["gggv","gggv","gvgv","gggv"]
ORDER = (
    "L L L L L L L T T Ts Ts T T T Ts Ts Qs T P P P P P P P P P P P P K K T T Ts Ts T T Qs T "
    "Q Ts Ts Qs Q M Qs M M T P P P P P P P P P P P P K K T T X X Ts Ts F Fs X X X F Fs X T T "
    "Q Q Es M T Ts X X X Ts X X F F Fs F Fs F Es M Es M Es Es M M Es M T P P P P P P P P P P P "
    "P K K T T Ts Ts T T X Es M Es M Es Es M M T Ts Ts F Fs F Fv X X Es M Es M Es M Es M T P P P P "
    "P P P P P P P P K K Es M Ws X X Es M Es M Es M Es M Es M Es M Es M Es M Es M F F Fv F Fv F Es "
    "M Es Es Es M M M Es M Es M Es M Es M Es M Es M Es M Es M Wv W O Es M Es M Es M Wv W O Wv Es M Es M "
    "Es M Es M Es M Es M W O Wv Es M Es M Es M W O Zs Zs Zs Zs Wv W O Wv W O Wv Es M Es Es Es M M M Es M "
    "Es M Es M W O Wv Es M Es M Es M W O Zs Zs Zs Zs Wv W O Wv W O Es M Es M Es M Es Es Es Wv W O Wv W O "
    "Zs Zs Zs Zs Wv W O Wv W O Wv W O W O Zs Zs Zs Zs "
)


def tile_plgmultiheadattention_pa_v_kernel(tc, q, Wq, bq, G, rope_cos, rope_sin, grad_out, out_0, out_1):
    nc = tc.nc

    go_view = grad_out.rearrange("b h (p j) e -> (b h) p j e", j=PACK)
    g_view = G.rearrange("h (r m) e -> h r m e", m=PACK)
    cos_view = rope_cos.rearrange("(p j) i -> p j i", j=PACK)
    sin_view = rope_sin.rearrange("(p j) i -> p j i", j=PACK)
    q_view = q.rearrange("b (p j) c -> (b p) j c", j=PACK)
    w_view = Wq.rearrange("(g p j) c -> g p j c", g=H, j=PACK)
    dw_view = out_1.rearrange("(h a i u) c -> h u a i c", h=H, a=2, u=2)
    dq_view = out_0.rearrange("b (p j) c -> j (b p) c", j=PACK)

    with ExitStack() as ctx:
        keep = ctx.enter_context(tc.tile_pool(name="keep", bufs=1))
        region = ctx.enter_context(tc.tile_pool(name="region", bufs=1))
        sb = ctx.enter_context(tc.tile_pool(name="sb", bufs=2))
        psum = ctx.enter_context(tc.psum_pool(name="psum", bufs=2))
        ctx.enter_context(tc.manual_schedule())

        ident = keep.tile([P, P], F32, name="ident")
        tab = keep.tile([P, 2, PACK, PAIRS], F32, name="tab")
        q_codes = keep.tile([P, D], U32, name="q_codes", align_bytes=64)
        q_scales = keep.tile([P, D], U8, name="q_scales", align_bytes=64)
        w_codes = keep.tile([P, H, D], U32, name="w_codes", align_bytes=64)
        w_scales = keep.tile([P, H, D], U8, name="w_scales", align_bytes=64)
        f_codes = keep.tile([P, H, S], U32, name="f_codes", align_bytes=64)
        f_scales = keep.tile([P, H, S], U8, name="f_scales", align_bytes=64)

        raw = {}

        def load_head(h):
            name = "head%d" % h
            t = region.tile([P, 2, PACK, DH], BF16, name=name, tag=name, offset=KIB * (32 + 8 * h))
            if h == 0:
                nc.sync.dma_start(out=t[:, 0, 0:2, :], in_=go_view[h, :, 0:2, :])
                nc.sync.dma_start(out=t[:, 0, 2:4, :], in_=go_view[h, :, 2:4, :])
            else:
                nc.sync.dma_start(out=t[:, 0, :, :], in_=go_view[h])
            nc.sync.dma_start(out=t[:, 1, :, :], in_=g_view[h])
            raw["go", h] = t[:, 0, :, :]
            raw["g", h] = t[:, 1, :, :]

        def load_q(half):
            name = "q%d" % half
            t = region.tile([P, PACK, 1024], BF16, name=name, tag=name, offset=KIB * 8 * half)
            nc.sync.dma_start(out=t[:], in_=q_view[:, :, half * 1024 : half * 1024 + 1024])
            raw["q", half] = t

        def load_w(g, j):
            if j == 0:
                name = "w%d" % g
                place = (0, 1, 2, 3)[g]
                raw["w", g] = region.tile([P, PACK, D], BF16, name=name, tag=name, offset=KIB * 16 * place)
            nc.sync.dma_start(out=raw["w", g][:, j, :], in_=w_view[g, :, j, :])

        def load_tab():
            nc.sync.dma_start(out=tab[:, 0, :, :], in_=cos_view)
            nc.sync.dma_start(out=tab[:, 1, :, :], in_=sin_view)

        def copy(engine, out, in_):
            if engine == "v":
                nc.vector.tensor_copy(out=out, in_=in_)
            else:
                nc.scalar.copy(out=out, in_=in_)

        def bank_of(blocks):
            bank = psum.tile([P, 4, P], F32, name="tp", tag="tp", bufs=2)
            for a in range(4):
                nc.tensor.transpose(bank[:, a, :], blocks[a], ident[:])
            return bank

        grouped = {}
        banks = {}
        codes = {}

        def turn_go(h, b):
            words = raw["go", h].rearrange("p j e -> p (j e)").bitcast(F32)
            blocks = [words[:, 256 * (2 * b + jj) + u : 256 * (2 * b + jj) + 256 : 2] for jj in range(2) for u in range(2)]
            banks["go", b] = bank_of(blocks)

        def out_go(h, b, engine):
            if b == 0:
                grouped["go", h] = sb.tile([P, S * PACK], BF16, name="grp_in", tag="grp_in", bufs=2, align_bytes=64)
            words_out("go", grouped["go", h], b, engine)

        def words_out(name, tile, b, engine):
            dst = tile[:].bitcast(F32)[:, 512 * b : 512 * b + 512]
            copy(
                engine,
                dst.rearrange("p (j r u) -> p j r u", j=2, u=2),
                banks[name, b][:].rearrange("p (j u) r -> p j r u", j=2),
            )

        def turn_g(h, b):
            words = raw["g", h].rearrange("p m e -> p (m e)").bitcast(F32)
            blocks = [words[:, 256 * (b + 2 * a) + u : 256 * (b + 2 * a) + 256 : 2] for a in range(2) for u in range(2)]
            banks["g", b] = bank_of(blocks)

        def out_g(h, b, engine):
            if b == 0:
                grouped["g", h] = sb.tile([P, DH * PACK], BF16, name="grp_in", tag="grp_in", bufs=2, align_bytes=64)
            dst = grouped["g", h][:].bitcast(F32)[:, 512 * b : 512 * b + 512]
            copy(engine, dst.rearrange("p (r a) -> p r a", a=4), banks["g", b][:].rearrange("p a r -> p r a"))

        def quant(key, dtype, out_codes=None, out_scales=None):
            nc.vector.quantize_mx(out=out_codes.bitcast(dtype), scales=out_scales, in_=grouped[key][:])

        def quant_in(name, h):
            c = sb.tile([P, 512], U32, name="c_" + name, tag="c_" + name, bufs=2, align_bytes=64)
            s = sb.tile([P, 512], U8, name="s_" + name, tag="s_" + name, bufs=2, align_bytes=64)
            quant((name, h), E5M2 if name == "go" else E4M3, c[:], s[:])
            codes[name, h] = (c, s)

        dr = {}

        def stage_one(h, j):
            gc, gs = codes["go", h]
            mc, ms = codes["g", h]
            bank = psum.tile([P, NT], F32, name="dr", tag="dr", bufs=3)
            cols = slice(P * j, P * j + P)
            nc.tensor.matmul_mx(
                out=bank[:], lhsT=gc[:, cols].bitcast(E5M2), lhsT_scale=gs[:, cols],
                rhs=mc[:].bitcast(E4M3), rhs_scale=ms[:], start=True, stop=True,
            )
            dr[h, j] = bank

        prods = {}
        dqp = {}

        def products(h, j):
            if j == 0:
                prods[h] = region.tile([P, PACK, 2, 2, PAIRS], F32, name="prods", tag="prods", offset=KIB * 64)
            bank = dr[h, j][:].rearrange("p (u i) -> p u i", u=2)
            nc.vector.tensor_tensor(
                out=prods[h][:, j, :, :, :],
                in0=bank.unsqueeze(1).to_broadcast([P, 2, 2, PAIRS]),
                in1=tab[:, :, j, :].unsqueeze(2).to_broadcast([P, 2, 2, PAIRS]),
                op=MULT,
            )

        def combine(h, j, engine):
            if j == 0:
                dqp[h] = sb.tile([P, PACK, 2, PAIRS], BF16, name="dqp", tag="dqp", bufs=2)
            pr = prods[h]
            e = nc.gpsimd if engine == "g" else nc.vector
            for u in range(2):
                e.tensor_tensor(
                    out=dqp[h][:, j, u, :], in0=pr[:, j, 0, u, :], in1=pr[:, j, 1, 1 - u, :], op=ADD if u == 0 else SUB
                )

        def group_tokens(h, engine):
            grouped["tok", h] = sb.tile([P, DH * PACK], BF16, name="grp_d", tag="grp_d", bufs=3, align_bytes=64)
            copy(
                engine,
                grouped["tok", h][:].rearrange("p (d j) -> p d j", j=PACK),
                dqp[h][:].rearrange("p j u i -> p (u i) j"),
            )

        def quant_tokens(h):
            c = sb.tile([P, 512], U32, name="c_tok", tag="c_tok", bufs=4, align_bytes=64)
            s = sb.tile([P, 512], U8, name="s_tok", tag="s_tok", bufs=4, align_bytes=64)
            quant(("tok", h), E5M2, c[:], s[:])
            codes["tok", h] = (c, s)

        def turn_dqp(h, b):
            words = dqp[h][:].rearrange("p j u i -> p (j u i)").bitcast(F32)
            banks["f", b] = bank_of([words[:, P * (4 * b + a) : P * (4 * b + a) + P] for a in range(4)])

        def out_dqp(h, b, engine):
            if b == 0:
                grouped["f", h] = sb.tile([P, S * PACK], BF16, name="grp_d", tag="grp_d", bufs=3, align_bytes=64)
            words_out("f", grouped["f", h], b, engine)

        def quant_features(h):
            quant(("f", h), E5M2, f_codes[:, h, :], f_scales[:, h, :])

        def group_q(n, engine):
            grouped["q", n] = sb.tile([P, NT * PACK], BF16, name="grp_w", tag="grp_w", bufs=3, align_bytes=64)
            src = raw["q", n // 2][:, :, NT * (n % 2) : NT * (n % 2) + NT]
            copy(engine, grouped["q", n][:].rearrange("p (c j) -> p c j", j=PACK), src.rearrange("p j c -> p c j"))

        def quant_q(n):
            cols = slice(NT * n, NT * n + NT)
            quant(("q", n), E4M3, q_codes[:, cols], q_scales[:, cols])

        def group_w(n, g, engine):
            grouped["w", n, g] = sb.tile([P, NT * PACK], BF16, name="grp_w", tag="grp_w", bufs=3, align_bytes=64)
            src = raw["w", g][:, :, NT * n : NT * n + NT]
            copy(
                engine,
                grouped["w", n, g][:].rearrange("p (c u e) -> p c u e", u=2, e=2),
                src.rearrange("p (e u) c -> p c u e", e=2),
            )

        def quant_w(n, g):
            cols = slice(NT * n, NT * n + NT)
            quant(("w", n, g), E4M3, w_codes[:, g, cols], w_scales[:, g, cols])

        stage = {}
        accs = {}

        def dw_mm(h, t, c, first, width):
            tc_, ts_ = codes["tok", h]
            acc = psum.tile([P, NT], F32, name="acc", tag="acc", bufs=3)
            rows = slice(P * t, P * t + P)
            cols = slice(c, c + NT)
            nc.tensor.matmul_mx(
                out=acc[:], lhsT=tc_[:, rows].bitcast(E5M2), lhsT_scale=ts_[:, rows],
                rhs=q_codes[:, cols].bitcast(E4M3), rhs_scale=q_scales[:, cols], start=True, stop=True,
            )
            accs[h, t, c] = acc

        def dw_out(h, t, c, first, width, engine):
            if c == first:
                stage[0] = sb.tile([P, width], F32, name="stage", tag="stage", bufs=3)
            copy(engine, stage[0][:, c - first : c - first + NT], accs[h, t, c][:])
            if c + NT == first + width:
                nc.sync.dma_start(out=dw_view[h, t // 2, t % 2, :, first : first + width], in_=stage[0][:])

        acc0 = {}

        def dq_mm(n, g):
            for j in range(PACK):
                if g == 1:
                    tag = "dr" if j < 3 else "tp"
                    acc0[n, j] = psum.tile([P, NT], F32, name=tag, tag=tag, bufs=3 if j < 3 else 2)
                rows = slice(P * j, P * j + P)
                cols = slice(NT * n, NT * n + NT)
                nc.tensor.matmul_mx(
                    out=acc0[n, j][:], lhsT=f_codes[:, g, rows].bitcast(E5M2), lhsT_scale=f_scales[:, g, rows],
                    rhs=w_codes[:, g, cols].bitcast(E4M3), rhs_scale=w_scales[:, g, cols], start=g == 1, stop=g == 3,
                )

        def dq_out(n, j, engine):
            name = "dq%d" % (4 * (n % 2) + j)
            t = region.tile([P, NT], F32, name=name, tag=name, offset=KIB * (64 + 8 * (n % 2) + 2 * j))
            copy(engine, t[:], acc0[n, j][:])
            nc.sync.dma_start(out=dq_view[j, :, NT * n : NT * n + NT], in_=t[:])

        make_identity(nc, ident[:])
        gs = (1, 2, 0, 3)
        steps = {
            "L": [(load_head, 0)] + [(load_tab,), (load_q, 0), (load_head, 1), (load_q, 1)] + [(load_head, 2), (load_head, 3)],
            "T": [], "P": [], "K": [], "F": [], "Q": [], "W": [], "M": [], "E": [], "O": [], "Z": [], "X": [],
        }
        for h in range(H):
            steps["T"] += [(turn_go, h, 0), (turn_go, h, 1), (out_go, h, 0), (out_go, h, 1), (turn_g, h, 0), (turn_g, h, 1)]
            steps["T"] += [(quant_in, "go", h), (out_g, h, 0), (out_g, h, 1), (quant_in, "g", h)]
            steps["P"] += [(stage_one, h, 0), (stage_one, h, 1), (stage_one, h, 2)]
            for j in range(PACK):
                steps["P"].append((products, h, j))
                if j == 0:
                    steps["P"].append((stage_one, h, 3))
                steps["P"].append((combine, h, j, ADDS[h][j]))
            steps["K"] += [(group_tokens, h, "v"), (quant_tokens, h)]
            steps["F"] += [(turn_dqp, h, 0), (out_dqp, h, 0), (turn_dqp, h, 1), (out_dqp, h, 1), (quant_features, h)]
            width = 1024 if h == 0 else D
            for first in range(0, D, width):
                for t in range(4):
                    for c in range(first, first + width, NT):
                        steps["M"].append((dw_mm, h, t, c, first, width))
                        steps["E"].append((dw_out, h, t, c, first, width))
        steps["Q"] = [(group_q, 0), (group_q, 1), (quant_q, 0), (group_q, 2), (quant_q, 1), (group_q, 3), (quant_q, 2), (quant_q, 3)]
        ws = [(n, g) for n in range(4) for g in gs]
        steps["W"].append((group_w,) + ws[0])
        for k in range(16):
            if k < 15:
                steps["W"].append((group_w,) + ws[k + 1])
            steps["W"].append((quant_w,) + ws[k])
            steps["O"].append((dq_mm,) + ws[k])
        steps["Z"] = [(dq_out, n, j) for n in range(4) for j in range(4)]
        steps["X"] = [(load_w, g, j) for g in gs for j in range(4)]
        for token in ORDER.split():
            step = steps[token[0]].pop(0)
            step[0](*step[1:], *token[1:])
